import numpy as np
import ml_dtypes


def mxq(x, axis, fmt="e4m3"):
    dtype, down = {"e4m3": (ml_dtypes.float8_e4m3fn, 7), "e5m2": (ml_dtypes.float8_e5m2, 14)}[fmt]
    v = np.moveaxis(np.asarray(x, np.float32).astype(ml_dtypes.bfloat16).astype(np.float64), axis, -1)
    blocks = v.reshape(v.shape[:-1] + (-1, 32))
    amax = np.abs(blocks).max(-1, keepdims=True)
    byte = np.maximum(np.where(amax > 0, np.frexp(amax)[1] - 1 + 127, 0) - down, 1)
    scale = np.exp2(byte - 127.0)
    codes = (blocks / scale).astype(np.float32).astype(dtype).astype(np.float64)
    return np.moveaxis((codes * scale).reshape(v.shape), -1, axis)


WIDE = False


def mx_kscale(k):
    if not WIDE:
        return np.ones(k)
    levels = np.array([10, -10, 5, -5, 0])
    if k % 512:
        return np.exp2(np.random.permutation(np.resize(levels, k // 32))).repeat(32)
    a = np.empty((k // 512, 16))
    for p in range(k // 512):
        a[p, :8] = np.random.permutation(np.resize(levels, 8))
        for g in range(8):
            far = levels[np.abs(levels - a[p, g]) >= 10]
            a[p, g + 8] = far[np.random.randint(len(far))]
    return np.exp2(a.ravel()).repeat(32)


BF16 = ml_dtypes.bfloat16


def bf(x):
    return np.asarray(x, np.float32).astype(BF16)


def f64(x):
    return np.asarray(x).astype(np.float64)


E2M1 = np.array([0.0, 0.5, 1.0, 1.5, 2.0, 3.0, 4.0, 6.0, -0.0, -0.5, -1.0, -1.5, -2.0, -3.0, -4.0, -6.0])


def pack_weight(w, fmt):
    k, n = w.shape
    w = f64(bf(w)).reshape(k // 32, 32, n)
    amax = np.abs(w).max(1)
    if fmt == "e4m3":
        byte = np.frexp(amax)[1] - 1 + 127 - 7
    else:
        mant, ex = np.frexp(amax / 6.0)
        byte = np.where(mant > 0.5, ex, ex - 1) + 127
    byte = np.clip(np.where(amax > 0, byte, 1), 1, 254)
    scaled = (w * np.exp2(127.0 - byte)[:, None, :]).reshape(k, n).astype(np.float32)
    by_word = np.ascontiguousarray(scaled.reshape(k // 512, 128, 4, n).transpose(0, 1, 3, 2))
    if fmt == "e4m3":
        words = by_word.astype(ml_dtypes.float8_e4m3fn).view(np.uint8)
    else:
        c = by_word.astype(ml_dtypes.float4_e2m1fn).view(np.uint8) & 0xF
        words = c[..., 0::2] | (c[..., 1::2] << 4)
    return np.ascontiguousarray(words), np.ascontiguousarray(byte.astype(np.uint8).reshape(k // 512, 16, n))


def unpack_weight(words, scales, fmt):
    g, p, n, _ = words.shape
    if fmt == "e4m3":
        vals = np.ascontiguousarray(words).view(ml_dtypes.float8_e4m3fn).astype(np.float64)
    else:
        nib = np.empty((g, p, n, 4), np.uint8)
        nib[..., 0::2] = words & 0xF
        nib[..., 1::2] = words >> 4
        vals = E2M1[nib]
    vals = vals * np.repeat(np.exp2(scales.astype(np.float64) - 127.0), 8, axis=1)[..., None]
    return vals.transpose(0, 1, 3, 2).reshape(g * 512, n)
def pack4(w):
    words, scales = pack_weight(w, "e2m1")
    return words.reshape(words.shape[0], 128, -1), scales


def unpack4(words, scales):
    return unpack_weight(words.reshape(words.shape[0], 128, -1, 2), scales, "e2m1")


SL, BS, DM, H, NH, DO = 32, 128, 1024, 16, 64, 1024
DP = H * NH


def draw0():
    s, t = mx_kscale(DM), mx_kscale(DP)
    g = np.random.standard_normal((SL, BS, H)) * 2.0
    values = bf(np.random.standard_normal((SL, BS, DM)) * s)
    logw = bf(g - np.log(np.exp(g).sum(0, keepdims=True)))
    Wv_words, Wv_scales = pack4((np.random.standard_normal((DP, DM)) / np.sqrt(DM * SL) / s * t[:, None]).T)
    Wo_words, Wo_scales = pack4((np.random.standard_normal((DO, DP)) * 0.5 / np.sqrt(DP) / t).T)
    return {"values": values,
            "logw": logw,
            "Wv_words": Wv_words, "Wv_scales": Wv_scales,
            "Wo_words": Wo_words, "Wo_scales": Wo_scales}


def core(values, logw, Wv_words, Wv_scales, Wo_words, Wo_scales):
    vp = mxq(f64(values), 2, "e4m3") @ unpack4(Wv_words, Wv_scales)
    attn = (f64(logw)[..., None] * vp.reshape(SL, BS, H, NH)).sum(0)
    return mxq(attn.reshape(BS, DP), 1, "e4m3") @ unpack4(Wo_words, Wo_scales)


def e4m3fn_bytes(y):
    return np.clip(np.asarray(y, np.float64), -448.0, 448.0).astype(np.float32).astype(ml_dtypes.float8_e4m3fn).view(np.uint8)


def e4m3fn_values(b):
    return np.asarray(b, np.uint8).view(ml_dtypes.float8_e4m3fn).astype(np.float64)


def setup_inputs():
    d = draw0()
    x0 = np.asarray(d['values']).astype(np.float64)
    s = (np.max(np.abs(x0), axis=(0, 1), keepdims=True) / 448.0).astype(np.float32)
    out = {}
    for k, v in d.items():
        if k == 'values':
            out['values_bytes'] = e4m3fn_bytes(x0 / s.astype(np.float64))
            out['values_scale'] = s
        else:
            out[k] = v
    return out


def reference(values_bytes, values_scale, logw, Wv_words, Wv_scales, Wo_words, Wo_scales):
    return core(e4m3fn_values(values_bytes) * values_scale.astype(np.float64), logw, Wv_words, Wv_scales, Wo_words, Wo_scales)

@@ -1,0 +1,296 @@
+from contextlib import ExitStack
+
+import concourse.mybir as mybir
+from concourse.masks import make_identity
+
+F32 = mybir.dt.float32
+BF16 = mybir.dt.bfloat16
+U32 = mybir.dt.uint32
+I32 = mybir.dt.int32
+U8 = mybir.dt.uint8
+FP8 = mybir.dt.float8_e4m3fn
+FP8X4 = mybir.dt.float8_e4m3fn_x4
+FP4X4 = mybir.dt.float4_e2m1fn_x4
+MULT = mybir.AluOpType.mult
+ADD = mybir.AluOpType.add
+SUB = mybir.AluOpType.subtract
+AXIS_X = mybir.AxisListType.X
+
+S, B, D, H = 32, 128, 1024, 16
+P = 128
+G = 2
+NT = 32
+BF = 4
+NB = 8
+TB = 8
+
+FLOPS = 2 * S * B * D * D + 2 * B * D * D
+
+
+def tile_multiheadattention_pb_w4_kernel(
+    tc, values_bytes, values_scale, logw, Wv_words, Wv_scales, Wo_words, Wo_scales, out
+):
+    nc = tc.nc
+    with ExitStack() as ctx:
+        keep = ctx.enter_context(tc.tile_pool(name="keep", bufs=1))
+        stage = ctx.enter_context(tc.tile_pool(name="stage", bufs=3))
+        psum = ctx.enter_context(tc.psum_pool(name="psum", bufs=2))
+        ctx.enter_context(tc.manual_schedule())
+
+        scale_sb = keep.tile([P, D], F32, name="scale_sb")
+        logw_sb = keep.tile([P, NT * H], BF16, name="logw_sb")
+        wv = keep.tile([P, G, 2 * D], U8, name="wv", align_bytes=64)
+        wo = keep.tile([P, G, 2 * D], U8, name="wo", align_bytes=64)
+        wv_sc = keep.tile([P, G, D], U8, name="wv_sc", align_bytes=64)
+        wo_sc = keep.tile([P, G, D], U8, name="wo_sc", align_bytes=64)
+        ident = keep.tile([P, P], F32, name="ident", align_bytes=64)
+        mask = keep.tile([P, BF], F32, name="mask")
+        lw = keep.tile([P, BF, NT, NB, 2], BF16, name="lw", align_bytes=64)
+        perm = keep.tile([P, 4, 224], BF16, name="perm", align_bytes=64)
+        attn_t = keep.tile([P, NB, B], BF16, name="attn_t", align_bytes=64)
+        attn_k = keep.tile([P, G, B, 4], BF16, name="attn_k", align_bytes=64)
+        attn_codes = keep.tile([P, G * B], U32, name="attn_codes", align_bytes=64)
+        attn_sc = keep.tile([P, G * B], U8, name="attn_sc", align_bytes=64)
+
+        nc.gpsimd.memset(wv_sc[:].rearrange("p g n -> p (g n)").bitcast(I32), 0)
+        make_identity(nc, ident[:])
+        nc.gpsimd.memset(wo_sc[:].rearrange("p g n -> p (g n)").bitcast(I32), 0)
+        nc.gpsimd.memset(perm[:], 0.0)
+
+        tokens = values_bytes.flatten_outer_dims().rearrange("(i c) k -> i c k", c=NT)
+        chunks = [(0, 2), (2, 4), (4, 8), (8, 12), (12, 16), (16, 20), (20, 24), (24, 28), (28, 32)]
+        vbytes = {}
+
+        def load_values(k):
+            c0, c1 = chunks[k]
+            vb = keep.tile([P, c1 - c0, D], U8, name="vb%d" % k, align_bytes=64)
+            nc.sync.dma_start(out=vb[:], in_=tokens[:, c0:c1, :])
+            for c in range(c0, c1):
+                vbytes[c] = vb[:, c - c0, :]
+
+        def load_scales(dst, src):
+            d = dst[:].bitcast(I32)
+            s = src.bitcast(I32)
+            for r in range(4):
+                nc.sync.dma_start(out=d[r:P:32, :, :], in_=s[:, r::4, :].rearrange("g q n -> q g n"))
+
+        nc.sync.dma_start(
+            out=scale_sb[:], in_=values_scale.rearrange("a o k -> (a o k)").partition_broadcast(P)
+        )
+        load_values(0)
+        nc.sync.dma_start(
+            out=logw_sb[:],
+            in_=logw.flatten_outer_dims().rearrange("(i c) h -> i (c h)", c=NT),
+        )
+        nc.sync.dma_start(out=wv[:], in_=Wv_words.rearrange("g p x -> p g x"))
+        load_scales(wv_sc, Wv_scales)
+        for k in range(1, len(chunks)):
+            load_values(k)
+        nc.sync.dma_start(out=wo[:], in_=Wo_words.rearrange("g p x -> p g x"))
+        load_scales(wo_sc, Wo_scales)
+
+        xs = {}
+        trs = {}
+        grouped = {}
+        codes = {}
+        scs = {}
+        vps = {}
+        his = {}
+        los = {}
+        pools = {}
+        perms = {}
+
+        def widen(c):
+            x = stage.tile([P, D], BF16, name="x", bufs=8, align_bytes=64)
+            nc.vector.tensor_tensor(out=x[:], in0=vbytes[c].bitcast(FP8), in1=scale_sb[:], op=MULT)
+            xs[c] = x
+
+        def turn(c):
+            tr = psum.tile([P, 4, P], F32, name="tr", bufs=2)
+            words = xs[c][:].bitcast(F32)
+            for g in range(G):
+                for u in range(2):
+                    nc.tensor.transpose(
+                        tr[:, 2 * g + u, :], words[:, 256 * g + u : 256 * (g + 1) : 2], ident[:]
+                    )
+            trs[c] = tr
+
+        def gather(c):
+            j, h = divmod(c, 2)
+            if h == 0:
+                gr = stage.tile([P, 2 * D], BF16, name="gr", bufs=3, align_bytes=64)
+                grouped[j] = gr
+            dst = grouped[j][:, D * h : D * (h + 1)].bitcast(F32)
+            nc.scalar.copy(
+                out=dst.rearrange("p (g r u) -> p g r u", g=G, u=2),
+                in_=trs[c][:].rearrange("p (g u) r -> p g r u", u=2),
+            )
+
+        def quant(j):
+            co = stage.tile([P, D // 2], U32, name="co", bufs=3, align_bytes=64)
+            sc = stage.tile([P, D // 2], U8, name="sc", bufs=3, align_bytes=64)
+            nc.vector.quantize_mx(out=co[:].bitcast(FP8X4), scales=sc[:], in_=grouped[j][:])
+            codes[j], scs[j] = co, sc
+
+        def project(c):
+            j, h = divmod(c, 2)
+            for n in range(2):
+                vp = psum.tile([P, 512], F32, name="vp", bufs=4)
+                for g in range(G):
+                    lo_col = 256 * h + 128 * g
+                    nc.tensor.matmul_mx(
+                        out=vp[:],
+                        lhsT=codes[j][:, lo_col : lo_col + 128].bitcast(FP8X4),
+                        lhsT_scale=scs[j][:, lo_col : lo_col + 128],
+                        rhs=wv[:, g, 1024 * n : 1024 * (n + 1)].bitcast(FP4X4),
+                        rhs_scale=wv_sc[:, g, 512 * n : 512 * (n + 1)],
+                        start=(g == 0),
+                        stop=(g == G - 1),
+                    )
+                vps[c, n] = vp
+
+        def split_hi(c):
+            hi = stage.tile([P, D], BF16, name="hi", bufs=3, align_bytes=64)
+            for n in range(2):
+                nc.scalar.copy(out=hi[:, 512 * n : 512 * (n + 1)], in_=vps[c, n][:])
+            his[c] = hi
+
+        def split_lo(c):
+            lo = stage.tile([P, D], BF16, name="lo", bufs=3, align_bytes=64)
+            for n in range(2):
+                cols = slice(512 * n, 512 * (n + 1))
+                nc.vector.tensor_tensor(out=lo[:, cols], in0=vps[c, n][:], in1=his[c][:, cols], op=SUB)
+            los[c] = lo
+
+        def pool(c):
+            bt, cc = divmod(c, TB)
+            if cc == 0:
+                po = psum.tile([P, TB, NB, BF, 2], F32, name="po", bufs=2)
+                pools[bt] = po
+            for b in range(NB):
+                ch = slice(128 * b, 128 * (b + 1))
+                for part, start in ((his, True), (los, False)):
+                    nc.tensor.matmul(
+                        pools[bt][:, cc, b, :, :],
+                        lhsT=part[c][:, ch],
+                        rhs=lw[:, :, c, b, :],
+                        start=start,
+                        stop=not start,
+                    )
+
+        def pick(bt):
+            for hh in range(2):
+                rows = slice(64 * hh, 64 * (hh + 1))
+                dst = attn_t[rows, :, :].rearrange("q b (f c) -> q b f c", f=BF)
+                nc.scalar.copy(
+                    out=dst[:, :, :, TB * bt : TB * (bt + 1)],
+                    in_=pools[bt][rows, :, :, :, hh].rearrange("q c b f -> q b f c"),
+                )
+
+        def permute(bt):
+            pe = psum.tile([P, 4, G, BF, TB], F32, name="tr", bufs=2)
+            src = attn_t[:].rearrange("q (g j) (f c) -> q j g f c", g=G, f=BF)
+            for t in range(4):
+                for j in range(4):
+                    nc.tensor.matmul(
+                        pe[:, t, :, :, :],
+                        lhsT=perm[:, t, 96 - 32 * j : 224 - 32 * j],
+                        rhs=src[:, j, :, :, TB * bt : TB * (bt + 1)],
+                        start=(j == 0),
+                        stop=(j == 3),
+                    )
+            perms[bt] = pe
+
+        def interleave(bt):
+            dst = attn_k[:].rearrange("p g (f c) t -> p (g f) c t", f=BF)
+            nc.scalar.copy(
+                out=dst[:, :, TB * bt : TB * (bt + 1), :],
+                in_=perms[bt][:].rearrange("p t g f c -> p (g f) c t"),
+            )
+
+        nc.scalar.copy(out=perm[:, :, 96:128], in_=ident[:].rearrange("q (r t) -> q t r", t=4))
+        nc.vector.tensor_reduce(
+            out=mask[:], in_=ident[:].rearrange("p (q f) -> p f q", f=BF), axis=AXIS_X, op=ADD
+        )
+        widen(0)
+        widen(1)
+        turn(0)
+        turn(1)
+        gather(0)
+        gather(1)
+        for f in range(BF):
+            nc.vector.tensor_scalar(
+                out=lw[:, f, :, :, :].rearrange("p c b h -> p (c b h)"),
+                in0=logw_sb[:],
+                scalar1=mask[:, f : f + 1],
+                scalar2=None,
+                op0=MULT,
+            )
+        widen(2)
+        widen(3)
+        turn(2)
+        turn(3)
+        quant(0)
+        widen(4)
+        widen(5)
+        gather(2)
+        gather(3)
+
+        NJ = NT // 2
+        for j in range(NJ):
+            c = 2 * j
+            if j + 1 < NJ:
+                quant(j + 1)
+            project(c)
+            split_hi(c)
+            if c + 6 < NT:
+                widen(c + 6)
+            split_lo(c)
+            if j > 0:
+                pool(c - 1)
+                if c % TB == 0:
+                    pick(c // TB - 1)
+            if c + 4 < NT:
+                turn(c + 4)
+                turn(c + 5)
+            project(c + 1)
+            if c + 4 < NT:
+                gather(c + 4)
+            split_hi(c + 1)
+            if c + 7 < NT:
+                widen(c + 7)
+            split_lo(c + 1)
+            if c + 4 < NT:
+                gather(c + 5)
+            pool(c)
+            if j > 1 and c % TB == 2:
+                permute(c // TB - 1)
+                interleave(c // TB - 1)
+
+        pool(NT - 1)
+        pick(3)
+        permute(3)
+        interleave(3)
+        nc.vector.quantize_mx(
+            out=attn_codes[:].bitcast(FP8X4),
+            scales=attn_sc[:],
+            in_=attn_k[:].rearrange("p g b t -> p (g b t)"),
+        )
+        for n in range(2):
+            acc = psum.tile([P, 512], F32, name="vp", bufs=4)
+            for g in range(G):
+                nc.tensor.matmul_mx(
+                    out=acc[:],
+                    lhsT=attn_codes[:, 128 * g : 128 * (g + 1)].bitcast(FP8X4),
+                    lhsT_scale=attn_sc[:, 128 * g : 128 * (g + 1)],
+                    rhs=wo[:, g, 1024 * n : 1024 * (n + 1)].bitcast(FP4X4),
+                    rhs_scale=wo_sc[:, g, 512 * n : 512 * (n + 1)],
+                    start=(g == 0),
+                    stop=(g == G - 1),
+                )
+            res = keep.tile([P, 512], F32, name="res%d" % n)
+            if n == 0:
+                nc.scalar.copy(out=res[:], in_=acc[:])
+            else:
+                nc.vector.tensor_copy(out=res[:], in_=acc[:])
+            nc.sync.dma_start(out=out[:, 512 * n : 512 * (n + 1)], in_=res[:])

@@ -22,7 +22,9 @@ G = 2
 NT = 32
 BF = 4
 NB = 8
-TB = 8
+BATCHES = ((0, 8), (8, 16), (16, 24), (24, 30), (30, 32))
+ON_POOL = (3, 5, 8, 10, 13, 16, 20, 23, 27, 29)
+LAG = 2
 
 FLOPS = 2 * S * B * D * D + 2 * B * D * D
 
@@ -38,6 +40,7 @@ def tile_multiheadattention_pb_w4_kernel(
         ctx.enter_context(tc.manual_schedule())
 
         scale_sb = keep.tile([P, D], F32, name="scale_sb")
+        scale_turned = keep.tile([P, D], F32, name="scale_turned")
         logw_sb = keep.tile([P, NT * H], BF16, name="logw_sb")
         wv = keep.tile([P, G, 2 * D], U8, name="wv", align_bytes=64)
         wo = keep.tile([P, G, 2 * D], U8, name="wo", align_bytes=64)
@@ -58,7 +61,7 @@ def tile_multiheadattention_pb_w4_kernel(
         nc.gpsimd.memset(perm[:], 0.0)
 
         tokens = values_bytes.flatten_outer_dims().rearrange("(i c) k -> i c k", c=NT)
-        chunks = [(0, 2), (2, 4), (4, 8), (8, 12), (12, 16), (16, 20), (20, 24), (24, 28), (28, 32)]
+        chunks = [(0, 1), (1, 2), (2, 4), (4, 8), (8, 12), (12, 16), (16, 20), (20, 24), (24, 28), (28, 32)]
         vbytes = {}
 
         def load_values(k):
@@ -74,17 +77,19 @@ def tile_multiheadattention_pb_w4_kernel(
             for r in range(4):
                 nc.sync.dma_start(out=d[r:P:32, :, :], in_=s[:, r::4, :].rearrange("g q n -> q g n"))
 
-        nc.sync.dma_start(
-            out=scale_sb[:], in_=values_scale.rearrange("a o k -> (a o k)").partition_broadcast(P)
-        )
+        scale_row = values_scale.rearrange("a o k -> (a o k)")
+        nc.sync.dma_start(out=scale_sb[:, :512], in_=scale_row[:512].partition_broadcast(P))
         load_values(0)
+        nc.sync.dma_start(out=scale_sb[:, 512:], in_=scale_row[512:].partition_broadcast(P))
+        load_values(1)
+        load_values(2)
         nc.sync.dma_start(
             out=logw_sb[:],
             in_=logw.flatten_outer_dims().rearrange("(i c) h -> i (c h)", c=NT),
         )
         nc.sync.dma_start(out=wv[:], in_=Wv_words.rearrange("g p x -> p g x"))
         load_scales(wv_sc, Wv_scales)
-        for k in range(1, len(chunks)):
+        for k in range(3, len(chunks)):
             load_values(k)
         nc.sync.dma_start(out=wo[:], in_=Wo_words.rearrange("g p x -> p g x"))
         load_scales(wo_sc, Wo_scales)
@@ -100,9 +105,27 @@ def tile_multiheadattention_pb_w4_kernel(
         pools = {}
         perms = {}
 
-        def widen(c):
-            x = stage.tile([P, D], BF16, name="x", bufs=8, align_bytes=64)
-            nc.vector.tensor_tensor(out=x[:], in0=vbytes[c].bitcast(FP8), in1=scale_sb[:], op=MULT)
+        def widen(c, parts=1):
+            x = stage.tile([P, D], BF16, name="x", bufs=12, align_bytes=64)
+            for n in range(parts):
+                cols = slice(D // parts * n, D // parts * (n + 1))
+                nc.vector.tensor_tensor(
+                    out=x[:, cols], in0=vbytes[c][:, cols].bitcast(FP8), in1=scale_sb[:, cols], op=MULT
+                )
+            xs[c] = x
+
+        def widen_on_pool(c):
+            xc = stage.tile([P, D], BF16, name="xc", bufs=6, align_bytes=64)
+            nc.scalar.copy(out=xc[:], in_=vbytes[c].bitcast(FP8))
+            x = stage.tile([P, D], BF16, name="xp", bufs=8, align_bytes=64)
+            for n in range(2):
+                cols = slice(512 * n, 512 * (n + 1))
+                nc.gpsimd.tensor_tensor(
+                    out=x[:, cols].rearrange("p (u q e) -> p u q e", u=2, e=2),
+                    in0=xc[:, cols].rearrange("p (q u e) -> p u q e", u=2, e=2),
+                    in1=scale_turned[:, cols].rearrange("p (u q e) -> p u q e", u=2, e=2),
+                    op=MULT,
+                )
             xs[c] = x
 
         def turn(c):
@@ -110,38 +133,35 @@ def tile_multiheadattention_pb_w4_kernel(
             words = xs[c][:].bitcast(F32)
             for g in range(G):
                 for u in range(2):
-                    nc.tensor.transpose(
-                        tr[:, 2 * g + u, :], words[:, 256 * g + u : 256 * (g + 1) : 2], ident[:]
-                    )
+                    if c in ON_POOL:
+                        pick_words = slice(256 * g + 128 * u, 256 * g + 128 * (u + 1))
+                    else:
+                        pick_words = slice(256 * g + u, 256 * (g + 1), 2)
+                    nc.tensor.transpose(tr[:, 2 * g + u, :], words[:, pick_words], ident[:])
             trs[c] = tr
 
         def gather(c):
-            j, h = divmod(c, 2)
-            if h == 0:
-                gr = stage.tile([P, 2 * D], BF16, name="gr", bufs=3, align_bytes=64)
-                grouped[j] = gr
-            dst = grouped[j][:, D * h : D * (h + 1)].bitcast(F32)
+            gr = stage.tile([P, D], BF16, name="gr", bufs=4, align_bytes=64)
             nc.scalar.copy(
-                out=dst.rearrange("p (g r u) -> p g r u", g=G, u=2),
+                out=gr[:].bitcast(F32).rearrange("p (g r u) -> p g r u", g=G, u=2),
                 in_=trs[c][:].rearrange("p (g u) r -> p g r u", u=2),
             )
+            grouped[c] = gr
 
-        def quant(j):
-            co = stage.tile([P, D // 2], U32, name="co", bufs=3, align_bytes=64)
-            sc = stage.tile([P, D // 2], U8, name="sc", bufs=3, align_bytes=64)
-            nc.vector.quantize_mx(out=co[:].bitcast(FP8X4), scales=sc[:], in_=grouped[j][:])
-            codes[j], scs[j] = co, sc
+        def quant(c):
+            co = stage.tile([P, G * P], U32, name="co", bufs=4, align_bytes=64)
+            sc = stage.tile([P, G * P], U8, name="sc", bufs=4, align_bytes=64)
+            nc.vector.quantize_mx(out=co[:].bitcast(FP8X4), scales=sc[:], in_=grouped[c][:])
+            codes[c], scs[c] = co, sc
 
         def project(c):
-            j, h = divmod(c, 2)
             for n in range(2):
                 vp = psum.tile([P, 512], F32, name="vp", bufs=4)
                 for g in range(G):
-                    lo_col = 256 * h + 128 * g
                     nc.tensor.matmul_mx(
                         out=vp[:],
-                        lhsT=codes[j][:, lo_col : lo_col + 128].bitcast(FP8X4),
-                        lhsT_scale=scs[j][:, lo_col : lo_col + 128],
+                        lhsT=codes[c][:, P * g : P * (g + 1)].bitcast(FP8X4),
+                        lhsT_scale=scs[c][:, P * g : P * (g + 1)],
                         rhs=wv[:, g, 1024 * n : 1024 * (n + 1)].bitcast(FP4X4),
                         rhs_scale=wv_sc[:, g, 512 * n : 512 * (n + 1)],
                         start=(g == 0),
@@ -150,61 +170,67 @@ def tile_multiheadattention_pb_w4_kernel(
                 vps[c, n] = vp
 
         def split_hi(c):
-            hi = stage.tile([P, D], BF16, name="hi", bufs=3, align_bytes=64)
+            hi = stage.tile([P, D], BF16, name="hi", bufs=5, align_bytes=64)
             for n in range(2):
                 nc.scalar.copy(out=hi[:, 512 * n : 512 * (n + 1)], in_=vps[c, n][:])
             his[c] = hi
 
         def split_lo(c):
-            lo = stage.tile([P, D], BF16, name="lo", bufs=3, align_bytes=64)
+            lo = stage.tile([P, D], BF16, name="lo", bufs=5, align_bytes=64)
             for n in range(2):
                 cols = slice(512 * n, 512 * (n + 1))
                 nc.vector.tensor_tensor(out=lo[:, cols], in0=vps[c, n][:], in1=his[c][:, cols], op=SUB)
             los[c] = lo
 
+        batch_of = {c: bt for bt, (c0, c1) in enumerate(BATCHES) for c in range(c0, c1)}
+
         def pool(c):
-            bt, cc = divmod(c, TB)
-            if cc == 0:
-                po = psum.tile([P, TB, NB, BF, 2], F32, name="po", bufs=2)
+            bt = batch_of[c]
+            c0, c1 = BATCHES[bt]
+            if c == c0:
+                po = psum.tile([P, c1 - c0, NB, BF, 2], F32, name="po", bufs=2)
                 pools[bt] = po
             for b in range(NB):
                 ch = slice(128 * b, 128 * (b + 1))
                 for part, start in ((his, True), (los, False)):
                     nc.tensor.matmul(
-                        pools[bt][:, cc, b, :, :],
+                        pools[bt][:, c - c0, b, :, :],
                         lhsT=part[c][:, ch],
                         rhs=lw[:, :, c, b, :],
                         start=start,
                         stop=not start,
                     )
 
-        def pick(bt):
+        def pick(bt, copy):
+            c0, c1 = BATCHES[bt]
             for hh in range(2):
                 rows = slice(64 * hh, 64 * (hh + 1))
                 dst = attn_t[rows, :, :].rearrange("q b (f c) -> q b f c", f=BF)
-                nc.scalar.copy(
-                    out=dst[:, :, :, TB * bt : TB * (bt + 1)],
+                copy(
+                    out=dst[:, :, :, c0:c1],
                     in_=pools[bt][rows, :, :, :, hh].rearrange("q c b f -> q b f c"),
                 )
 
         def permute(bt):
-            pe = psum.tile([P, 4, G, BF, TB], F32, name="tr", bufs=2)
+            c0, c1 = BATCHES[bt]
+            pe = psum.tile([P, 4, G, BF, c1 - c0], F32, name="tr", bufs=2)
             src = attn_t[:].rearrange("q (g j) (f c) -> q j g f c", g=G, f=BF)
             for t in range(4):
                 for j in range(4):
                     nc.tensor.matmul(
                         pe[:, t, :, :, :],
                         lhsT=perm[:, t, 96 - 32 * j : 224 - 32 * j],
-                        rhs=src[:, j, :, :, TB * bt : TB * (bt + 1)],
+                        rhs=src[:, j, :, :, c0:c1],
                         start=(j == 0),
                         stop=(j == 3),
                     )
             perms[bt] = pe
 
-        def interleave(bt):
+        def interleave(bt, copy):
+            c0, c1 = BATCHES[bt]
             dst = attn_k[:].rearrange("p g (f c) t -> p (g f) c t", f=BF)
-            nc.scalar.copy(
-                out=dst[:, :, TB * bt : TB * (bt + 1), :],
+            copy(
+                out=dst[:, :, c0:c1, :],
                 in_=perms[bt][:].rearrange("p t g f c -> p (g f) c t"),
             )
 
@@ -212,65 +238,59 @@ def tile_multiheadattention_pb_w4_kernel(
         nc.vector.tensor_reduce(
             out=mask[:], in_=ident[:].rearrange("p (q f) -> p f q", f=BF), axis=AXIS_X, op=ADD
         )
-        widen(0)
-        widen(1)
-        turn(0)
-        turn(1)
-        gather(0)
-        gather(1)
-        for f in range(BF):
-            nc.vector.tensor_scalar(
-                out=lw[:, f, :, :, :].rearrange("p c b h -> p (c b h)"),
-                in0=logw_sb[:],
-                scalar1=mask[:, f : f + 1],
-                scalar2=None,
-                op0=MULT,
-            )
-        widen(2)
-        widen(3)
-        turn(2)
-        turn(3)
-        quant(0)
-        widen(4)
-        widen(5)
-        gather(2)
-        gather(3)
+        nc.gpsimd.tensor_copy(
+            out=scale_turned[:].rearrange("p (g u q e) -> p g u q e", g=G, u=2, e=2),
+            in_=scale_sb[:].rearrange("p (g q u e) -> p g u q e", g=G, u=2, e=2),
+        )
 
-        NJ = NT // 2
-        for j in range(NJ):
-            c = 2 * j
-            if j + 1 < NJ:
-                quant(j + 1)
-            project(c)
-            split_hi(c)
-            if c + 6 < NT:
-                widen(c + 6)
-            split_lo(c)
-            if j > 0:
-                pool(c - 1)
-                if c % TB == 0:
-                    pick(c // TB - 1)
-            if c + 4 < NT:
-                turn(c + 4)
-                turn(c + 5)
-            project(c + 1)
-            if c + 4 < NT:
-                gather(c + 4)
-            split_hi(c + 1)
-            if c + 7 < NT:
-                widen(c + 7)
-            split_lo(c + 1)
-            if c + 4 < NT:
-                gather(c + 5)
-            pool(c)
-            if j > 1 and c % TB == 2:
-                permute(c // TB - 1)
-                interleave(c // TB - 1)
+        def make_lw():
+            for f in range(BF):
+                nc.vector.tensor_scalar(
+                    out=lw[:, f, :, :, :].rearrange("p c b h -> p (c b h)"),
+                    in0=logw_sb[:],
+                    scalar1=mask[:, f : f + 1],
+                    scalar2=None,
+                    op0=MULT,
+                )
 
+        def wv_(c):
+            if 0 <= c < NT and c not in ON_POOL:
+                widen(c, 2 if c == 0 else 1)
+
+        def wp_(c):
+            if 0 <= c < NT and c in ON_POOL:
+                widen_on_pool(c)
+
+        def on(fn, c):
+            if 0 <= c < NT:
+                fn(c)
+
+        AW, AT, AG, AQ, AC = 5, 3, 2, 2, 9
+        for c in range(-12, NT):
+            if c == -6:
+                make_lw()
+            on(project, c)
+            on(gather, c + AG)
+            on(split_hi, c)
+            on(quant, c + AQ)
+            on(pool, c - LAG) if c >= LAG else None
+            wp_(c + AC)
+            on(turn, c + AT)
+            on(split_lo, c)
+            wv_(c + AW)
+            if c in (9, 17, 25):
+                pick((c - 9) // 8, nc.scalar.copy)
+            if c in (11, 19, 27):
+                permute((c - 11) // 8)
+                interleave((c - 11) // 8, nc.scalar.copy)
+        pick(3, nc.scalar.copy)
+        pool(NT - 2)
         pool(NT - 1)
-        pick(3)
+        pick(4, nc.vector.tensor_copy)
         permute(3)
-        interleave(3)
+        interleave(3, nc.scalar.copy)
+        permute(4)
+        interleave(4, nc.vector.tensor_copy)
         nc.vector.quantize_mx(
             out=attn_codes[:].bitcast(FP8X4),
             scales=attn_sc[:],

@@ -23,8 +23,9 @@ NT = 32
 BF = 4
 NB = 8
 BATCHES = ((0, 8), (8, 16), (16, 24), (24, 30), (30, 32))
-ON_POOL = (3, 5, 8, 10, 13, 16, 20, 23, 27, 29)
-LAG = 2
+PW = 768
+FIRST_SHARED = 3
+LAG = 3
 
 FLOPS = 2 * S * B * D * D + 2 * B * D * D
 
@@ -40,7 +41,6 @@ def tile_multiheadattention_pb_w4_kernel(
         ctx.enter_context(tc.manual_schedule())
 
         scale_sb = keep.tile([P, D], F32, name="scale_sb")
-        scale_turned = keep.tile([P, D], F32, name="scale_turned")
         logw_sb = keep.tile([P, NT * H], BF16, name="logw_sb")
         wv = keep.tile([P, G, 2 * D], U8, name="wv", align_bytes=64)
         wo = keep.tile([P, G, 2 * D], U8, name="wo", align_bytes=64)
@@ -80,13 +80,13 @@ def tile_multiheadattention_pb_w4_kernel(
         scale_row = values_scale.rearrange("a o k -> (a o k)")
         nc.sync.dma_start(out=scale_sb[:, :512], in_=scale_row[:512].partition_broadcast(P))
         load_values(0)
-        nc.sync.dma_start(out=scale_sb[:, 512:], in_=scale_row[512:].partition_broadcast(P))
-        load_values(1)
-        load_values(2)
         nc.sync.dma_start(
             out=logw_sb[:],
             in_=logw.flatten_outer_dims().rearrange("(i c) h -> i (c h)", c=NT),
         )
+        nc.sync.dma_start(out=scale_sb[:, 512:], in_=scale_row[512:].partition_broadcast(P))
+        load_values(1)
+        load_values(2)
         nc.sync.dma_start(out=wv[:], in_=Wv_words.rearrange("g p x -> p g x"))
         load_scales(wv_sc, Wv_scales)
         for k in range(3, len(chunks)):
@@ -95,6 +95,7 @@ def tile_multiheadattention_pb_w4_kernel(
         load_scales(wo_sc, Wo_scales)
 
         xs = {}
+        xcs = {}
         trs = {}
         grouped = {}
         codes = {}
@@ -105,43 +106,35 @@ def tile_multiheadattention_pb_w4_kernel(
         pools = {}
         perms = {}
 
-        def widen(c, parts=1):
-            x = stage.tile([P, D], BF16, name="x", bufs=12, align_bytes=64)
-            for n in range(parts):
-                cols = slice(D // parts * n, D // parts * (n + 1))
-                nc.vector.tensor_tensor(
-                    out=x[:, cols], in0=vbytes[c][:, cols].bitcast(FP8), in1=scale_sb[:, cols], op=MULT
-                )
+        def new_x(c):
+            x = stage.tile([P, D], BF16, name="x", bufs=14, align_bytes=64)
             xs[c] = x
 
+        def widen(c, c0=0, c1=D):
+            nc.vector.tensor_tensor(
+                out=xs[c][:, c0:c1], in0=vbytes[c][:, c0:c1].bitcast(FP8), in1=scale_sb[:, c0:c1], op=MULT
+            )
+
+        def cast(c):
+            xc = stage.tile([P, PW], BF16, name="xc", bufs=3, align_bytes=64)
+            nc.scalar.copy(out=xc[:], in_=vbytes[c][:, :PW].bitcast(FP8))
+            xcs[c] = xc
+
         def widen_on_pool(c):
-            xc = stage.tile([P, D], BF16, name="xc", bufs=6, align_bytes=64)
-            nc.scalar.copy(out=xc[:], in_=vbytes[c].bitcast(FP8))
-            x = stage.tile([P, D], BF16, name="xp", bufs=8, align_bytes=64)
-            for n in range(2):
-                cols = slice(512 * n, 512 * (n + 1))
-                nc.gpsimd.tensor_tensor(
-                    out=x[:, cols].rearrange("p (u q e) -> p u q e", u=2, e=2),
-                    in0=xc[:, cols].rearrange("p (q u e) -> p u q e", u=2, e=2),
-                    in1=scale_turned[:, cols].rearrange("p (u q e) -> p u q e", u=2, e=2),
-                    op=MULT,
-                )
-            xs[c] = x
+            nc.gpsimd.tensor_tensor(out=xs[c][:, :PW], in0=xcs[c][:], in1=scale_sb[:, :PW], op=MULT)
 
         def turn(c):
             tr = psum.tile([P, 4, P], F32, name="tr", bufs=2)
             words = xs[c][:].bitcast(F32)
             for g in range(G):
                 for u in range(2):
-                    if c in ON_POOL:
-                        pick_words = slice(256 * g + 128 * u, 256 * g + 128 * (u + 1))
-                    else:
-                        pick_words = slice(256 * g + u, 256 * (g + 1), 2)
-                    nc.tensor.transpose(tr[:, 2 * g + u, :], words[:, pick_words], ident[:])
+                    nc.tensor.transpose(
+                        tr[:, 2 * g + u, :], words[:, 256 * g + u : 256 * (g + 1) : 2], ident[:]
+                    )
             trs[c] = tr
 
         def gather(c):
-            gr = stage.tile([P, D], BF16, name="gr", bufs=4, align_bytes=64)
+            gr = stage.tile([P, D], BF16, name="gr", bufs=6, align_bytes=64)
             nc.scalar.copy(
                 out=gr[:].bitcast(F32).rearrange("p (g r u) -> p g r u", g=G, u=2),
                 in_=trs[c][:].rearrange("p (g u) r -> p g r u", u=2),
@@ -149,8 +142,8 @@ def tile_multiheadattention_pb_w4_kernel(
             grouped[c] = gr
 
         def quant(c):
-            co = stage.tile([P, G * P], U32, name="co", bufs=4, align_bytes=64)
-            sc = stage.tile([P, G * P], U8, name="sc", bufs=4, align_bytes=64)
+            co = stage.tile([P, G * P], U32, name="co", bufs=6, align_bytes=64)
+            sc = stage.tile([P, G * P], U8, name="sc", bufs=6, align_bytes=64)
             nc.vector.quantize_mx(out=co[:].bitcast(FP8X4), scales=sc[:], in_=grouped[c][:])
             codes[c], scs[c] = co, sc
 
@@ -170,13 +163,13 @@ def tile_multiheadattention_pb_w4_kernel(
                 vps[c, n] = vp
 
         def split_hi(c):
-            hi = stage.tile([P, D], BF16, name="hi", bufs=5, align_bytes=64)
+            hi = stage.tile([P, D], BF16, name="hi", bufs=6, align_bytes=64)
             for n in range(2):
                 nc.scalar.copy(out=hi[:, 512 * n : 512 * (n + 1)], in_=vps[c, n][:])
             his[c] = hi
 
         def split_lo(c):
-            lo = stage.tile([P, D], BF16, name="lo", bufs=5, align_bytes=64)
+            lo = stage.tile([P, D], BF16, name="lo", bufs=6, align_bytes=64)
             for n in range(2):
                 cols = slice(512 * n, 512 * (n + 1))
                 nc.vector.tensor_tensor(out=lo[:, cols], in0=vps[c, n][:], in1=his[c][:, cols], op=SUB)
@@ -238,54 +231,83 @@ def tile_multiheadattention_pb_w4_kernel(
         nc.vector.tensor_reduce(
             out=mask[:], in_=ident[:].rearrange("p (q f) -> p f q", f=BF), axis=AXIS_X, op=ADD
         )
-        nc.gpsimd.tensor_copy(
-            out=scale_turned[:].rearrange("p (g u q e) -> p g u q e", g=G, u=2, e=2),
-            in_=scale_sb[:].rearrange("p (g q u e) -> p g u q e", g=G, u=2, e=2),
-        )
-
-        def make_lw():
-            for f in range(BF):
-                nc.vector.tensor_scalar(
-                    out=lw[:, f, :, :, :].rearrange("p c b h -> p (c b h)"),
-                    in0=logw_sb[:],
-                    scalar1=mask[:, f : f + 1],
-                    scalar2=None,
-                    op0=MULT,
-                )
-
-        def wv_(c):
-            if 0 <= c < NT and c not in ON_POOL:
-                widen(c, 2 if c == 0 else 1)
-
-        def wp_(c):
-            if 0 <= c < NT and c in ON_POOL:
-                widen_on_pool(c)
+        for f in range(BF):
+            nc.scalar.activation(
+                out=lw[:, f, :, :, :].rearrange("p c b h -> p (c b h)"),
+                in_=logw_sb[:],
+                func=mybir.ActivationFunctionType.Copy,
+                scale=mask[:, f : f + 1],
+            )
 
         def on(fn, c):
             if 0 <= c < NT:
                 fn(c)
 
-        AW, AT, AG, AQ, AC = 5, 3, 2, 2, 9
-        for c in range(-12, NT):
-            if c == -6:
-                make_lw()
-            on(project, c)
-            on(gather, c + AG)
-            on(split_hi, c)
-            on(quant, c + AQ)
-            on(pool, c - LAG) if c >= LAG else None
-            wp_(c + AC)
-            on(turn, c + AT)
-            on(split_lo, c)
-            wv_(c + AW)
-            if c in (9, 17, 25):
-                pick((c - 9) // 8, nc.scalar.copy)
-            if c in (11, 19, 27):
-                permute((c - 11) // 8)
-                interleave((c - 11) // 8, nc.scalar.copy)
+        def both(fn, p, lead, shift=0):
+            for c in (2 * (p + lead) - shift, 2 * (p + lead) + 1 - shift):
+                if 0 <= c < NT:
+                    fn(c)
+
+        def products(p):
+            if 0 <= p < NT // 2:
+                widen(2 * p)
+                if p < FIRST_SHARED:
+                    widen(2 * p + 1)
+                else:
+                    widen(2 * p + 1, PW, D)
+
+        def shared(fn, p):
+            if FIRST_SHARED <= p < NT // 2:
+                fn(2 * p + 1)
+
+        def mark(c):
+            nc.vector.memset(xs[c][:, :16], 0.0)
+
+        for c in range(6):
+            new_x(c)
+        widen(0, 0, 512)
+        widen(0, 512, D)
+        widen(1)
+        turn(0)
+        gather(0)
+        turn(1)
+        gather(1)
+        widen(2)
+        quant(0)
+        widen(3)
+        quant(1)
+        project(0)
+        turn(2)
+        project(1)
+        turn(3)
+        split_hi(0)
+        gather(2)
+        split_hi(1)
+        gather(3)
+        widen(4)
+        widen(5)
+        cast(7)
+        for p in range(NT // 2):
+            both(new_x, p, 3)
+            both(project, p, 0) if p > 0 else None
+            both(turn, p, 2)
+            both(split_hi, p, 0) if p > 0 else None
+            both(gather, p, 2)
+            products(p + 3)
+            both(quant, p, 1)
+            shared(mark, p + 3)
+            shared(widen_on_pool, p + 3)
+            both(split_lo, p, 0)
+            shared(cast, p + 4)
+            both(pool, p, 0, 2)
+            if p in (4, 8, 12):
+                pick((p - 4) // 4, nc.scalar.copy)
+            if p in (5, 9, 13):
+                permute((p - 5) // 4)
+                interleave((p - 5) // 4, nc.scalar.copy)
         pick(3, nc.scalar.copy)
-        pool(NT - 2)
-        pool(NT - 1)
+        pool(30)
+        pool(31)
         pick(4, nc.vector.tensor_copy)
         permute(3)
         interleave(3, nc.scalar.copy)

@@ -16,18 +16,28 @@ ADD = mybir.AluOpType.add
 SUB = mybir.AluOpType.subtract
 AXIS_X = mybir.AxisListType.X
 
-S, B, D, H = 32, 128, 1024, 16
+SEQ, BATCH, D, HEADS = 32, 128, 1024, 16
+
 P = 128
 G = 2
+PASS = 512
+T = 4
 NT = 32
+PAIRS = NT // 2
 BF = 4
 NB = 8
-BATCHES = ((0, 8), (8, 16), (16, 24), (24, 30), (30, 32))
-PW = 768
-FIRST_SHARED = 3
-LAG = 3
+HB = 2
 
-FLOPS = 2 * S * B * D * D + 2 * B * D * D
+BATCHES = ((0, 6), (6, 12), (12, 18), (18, 24), (24, 30), (30, 32))
+
+POOL_BLOCKS = 3
+
+SCALED_LATE = (0, 1)
+
+FIRST_SHARED = 3
+SHARE = 640
+
+FLOPS = 2 * SEQ * BATCH * D * D + 2 * BATCH * D * D
 
 
 def tile_multiheadattention_pb_w4_kernel(
@@ -36,303 +46,284 @@ def tile_multiheadattention_pb_w4_kernel(
     nc = tc.nc
     with ExitStack() as ctx:
         keep = ctx.enter_context(tc.tile_pool(name="keep", bufs=1))
-        stage = ctx.enter_context(tc.tile_pool(name="stage", bufs=3))
+        stage = ctx.enter_context(tc.tile_pool(name="stage", bufs=6))
         psum = ctx.enter_context(tc.psum_pool(name="psum", bufs=2))
         ctx.enter_context(tc.manual_schedule())
 
-        scale_sb = keep.tile([P, D], F32, name="scale_sb")
-        logw_sb = keep.tile([P, NT * H], BF16, name="logw_sb")
+        factors = keep.tile([P, D], F32, name="factors")
+        factors_k = keep.tile([P, G, T], F32, name="factors_k")
+        logw_sb = keep.tile([P, NT * HEADS], BF16, name="logw_sb")
         wv = keep.tile([P, G, 2 * D], U8, name="wv", align_bytes=64)
         wo = keep.tile([P, G, 2 * D], U8, name="wo", align_bytes=64)
-        wv_sc = keep.tile([P, G, D], U8, name="wv_sc", align_bytes=64)
-        wo_sc = keep.tile([P, G, D], U8, name="wo_sc", align_bytes=64)
+        wv_scales = keep.tile([P, G, D], U8, name="wv_scales", align_bytes=64)
+        wo_scales = keep.tile([P, G, D], U8, name="wo_scales", align_bytes=64)
         ident = keep.tile([P, P], F32, name="ident", align_bytes=64)
-        mask = keep.tile([P, BF], F32, name="mask")
-        lw = keep.tile([P, BF, NT, NB, 2], BF16, name="lw", align_bytes=64)
-        perm = keep.tile([P, 4, 224], BF16, name="perm", align_bytes=64)
-        attn_t = keep.tile([P, NB, B], BF16, name="attn_t", align_bytes=64)
-        attn_k = keep.tile([P, G, B, 4], BF16, name="attn_k", align_bytes=64)
-        attn_codes = keep.tile([P, G * B], U32, name="attn_codes", align_bytes=64)
-        attn_sc = keep.tile([P, G * B], U8, name="attn_sc", align_bytes=64)
+        is_row = keep.tile([P, BF], F32, name="is_row")
+        weights = keep.tile([P, BF, NT, NB, HB], BF16, name="weights", align_bytes=64)
+        move = keep.tile([P, T, 224], BF16, name="move", align_bytes=64)
+        pooled = [
+            keep.tile([P, NB, BF, c1 - c0], BF16, name="pooled%d" % c0, align_bytes=64) for c0, c1 in BATCHES
+        ]
+        attn = keep.tile([P, G, BATCH, T], BF16, name="attn", align_bytes=64)
+        attn_codes = keep.tile([P, G * BATCH], U32, name="attn_codes", align_bytes=64)
+        attn_scales = keep.tile([P, G * BATCH], U8, name="attn_scales", align_bytes=64)
 
-        nc.gpsimd.memset(wv_sc[:].rearrange("p g n -> p (g n)").bitcast(I32), 0)
+        nc.gpsimd.memset(wv_scales[:].rearrange("p g n -> p (g n)").bitcast(I32), 0)
         make_identity(nc, ident[:])
-        nc.gpsimd.memset(wo_sc[:].rearrange("p g n -> p (g n)").bitcast(I32), 0)
-        nc.gpsimd.memset(perm[:], 0.0)
+        nc.gpsimd.memset(wo_scales[:].rearrange("p g n -> p (g n)").bitcast(I32), 0)
+        nc.gpsimd.memset(move[:], 0.0)
+        nc.vector.tensor_reduce(
+            out=is_row[:], in_=ident[:].rearrange("p (q f) -> p f q", f=BF), axis=AXIS_X, op=ADD
+        )
 
         tokens = values_bytes.flatten_outer_dims().rearrange("(i c) k -> i c k", c=NT)
-        chunks = [(0, 1), (1, 2), (2, 4), (4, 8), (8, 12), (12, 16), (16, 20), (20, 24), (24, 28), (28, 32)]
-        vbytes = {}
+        tile_bytes = {}
 
-        def load_values(k):
-            c0, c1 = chunks[k]
-            vb = keep.tile([P, c1 - c0, D], U8, name="vb%d" % k, align_bytes=64)
-            nc.sync.dma_start(out=vb[:], in_=tokens[:, c0:c1, :])
+        def load_values(c0, c1):
+            codes_in = keep.tile([P, c1 - c0, D], U8, name="codes_in%d" % c0, align_bytes=64)
+            nc.sync.dma_start(out=codes_in[:], in_=tokens[:, c0:c1, :])
             for c in range(c0, c1):
-                vbytes[c] = vb[:, c - c0, :]
+                tile_bytes[c] = codes_in[:, c - c0, :]
 
-        def load_scales(dst, src):
-            d = dst[:].bitcast(I32)
-            s = src.bitcast(I32)
+        def load_weight_scales(dst, src):
             for r in range(4):
-                nc.sync.dma_start(out=d[r:P:32, :, :], in_=s[:, r::4, :].rearrange("g q n -> q g n"))
+                nc.sync.dma_start(
+                    out=dst[:].bitcast(I32)[r:P:32, :, :],
+                    in_=src.bitcast(I32)[:, r::4, :].rearrange("g q n -> q g n"),
+                )
 
-        scale_row = values_scale.rearrange("a o k -> (a o k)")
-        nc.sync.dma_start(out=scale_sb[:, :512], in_=scale_row[:512].partition_broadcast(P))
-        load_values(0)
+        load_values(0, 1)
         nc.sync.dma_start(
-            out=logw_sb[:],
-            in_=logw.flatten_outer_dims().rearrange("(i c) h -> i (c h)", c=NT),
+            out=factors_k[:], in_=values_scale.rearrange("a o (g p t) -> p (a o g) t", g=G, t=T)
         )
-        nc.sync.dma_start(out=scale_sb[:, 512:], in_=scale_row[512:].partition_broadcast(P))
-        load_values(1)
-        load_values(2)
+        load_values(1, 2)
+        nc.sync.dma_start(
+            out=factors[:], in_=values_scale.rearrange("a o k -> (a o k)").partition_broadcast(P)
+        )
+        nc.sync.dma_start(
+            out=logw_sb[:], in_=logw.flatten_outer_dims().rearrange("(i c) h -> i (c h)", c=NT)
+        )
+        load_values(2, 4)
         nc.sync.dma_start(out=wv[:], in_=Wv_words.rearrange("g p x -> p g x"))
-        load_scales(wv_sc, Wv_scales)
-        for k in range(3, len(chunks)):
-            load_values(k)
+        load_weight_scales(wv_scales, Wv_scales)
+        for c0 in range(4, NT, 4):
+            load_values(c0, c0 + 4)
         nc.sync.dma_start(out=wo[:], in_=Wo_words.rearrange("g p x -> p g x"))
-        load_scales(wo_sc, Wo_scales)
+        load_weight_scales(wo_scales, Wo_scales)
 
-        xs = {}
-        xcs = {}
-        trs = {}
-        grouped = {}
-        codes = {}
-        scs = {}
-        vps = {}
-        his = {}
-        los = {}
-        pools = {}
-        perms = {}
+        product, plain, turned, grouped, codes, scales = {}, {}, {}, {}, {}, {}
+        vp, hi, lo, sums, moved = {}, {}, {}, {}, {}
 
-        def new_x(c):
+        def new_product(c):
             x = stage.tile([P, D], BF16, name="x", bufs=14, align_bytes=64)
-            xs[c] = x
+            product[c] = x
 
-        def widen(c, c0=0, c1=D):
+        def multiply(c, k0=0):
             nc.vector.tensor_tensor(
-                out=xs[c][:, c0:c1], in0=vbytes[c][:, c0:c1].bitcast(FP8), in1=scale_sb[:, c0:c1], op=MULT
+                out=product[c][:, k0:], in0=tile_bytes[c][:, k0:].bitcast(FP8), in1=factors[:, k0:], op=MULT
             )
 
-        def cast(c):
-            xc = stage.tile([P, PW], BF16, name="xc", bufs=3, align_bytes=64)
-            nc.scalar.copy(out=xc[:], in_=vbytes[c][:, :PW].bitcast(FP8))
-            xcs[c] = xc
+        def widen(c):
+            xc = stage.tile([P, SHARE], BF16, name="xc", bufs=3, align_bytes=64)
+            nc.scalar.copy(out=xc[:], in_=tile_bytes[c][:, :SHARE].bitcast(FP8))
+            plain[c] = xc
 
-        def widen_on_pool(c):
-            nc.gpsimd.tensor_tensor(out=xs[c][:, :PW], in0=xcs[c][:], in1=scale_sb[:, :PW], op=MULT)
+        def multiply_on_gpsimd(c):
+            nc.vector.memset(product[c][:, :16], 0.0)
+            nc.gpsimd.tensor_tensor(out=product[c][:, :SHARE], in0=plain[c][:], in1=factors[:, :SHARE], op=MULT)
 
         def turn(c):
-            tr = psum.tile([P, 4, P], F32, name="tr", bufs=2)
-            words = xs[c][:].bitcast(F32)
+            tr = psum.tile([P, 2 * G, P], F32, name="tr", bufs=2)
+            words = product[c][:].bitcast(F32)
             for g in range(G):
                 for u in range(2):
                     nc.tensor.transpose(
                         tr[:, 2 * g + u, :], words[:, 256 * g + u : 256 * (g + 1) : 2], ident[:]
                     )
-            trs[c] = tr
+            turned[c] = tr
 
         def gather(c):
-            gr = stage.tile([P, D], BF16, name="gr", bufs=6, align_bytes=64)
-            nc.scalar.copy(
-                out=gr[:].bitcast(F32).rearrange("p (g r u) -> p g r u", g=G, u=2),
-                in_=trs[c][:].rearrange("p (g u) r -> p g r u", u=2),
-            )
+            gr = stage.tile([P, D], BF16, name="gr", align_bytes=64)
+            if c in SCALED_LATE:
+                for g in range(G):
+                    values = turned[c][:, 2 * g : 2 * (g + 1), :].rearrange("p u r -> p (u r)").bitcast(BF16)
+                    factor = factors_k[:, g, :].unsqueeze(1).to_broadcast([P, P, T])
+                    nc.vector.tensor_tensor(
+                        out=gr[:, PASS * g : PASS * (g + 1)].rearrange("p (r u e) -> p r u e", u=2, e=2),
+                        in0=values.rearrange("p (u r e) -> p r u e", u=2, e=2),
+                        in1=factor.rearrange("p r (u e) -> p r u e", u=2),
+                        op=MULT,
+                    )
+            else:
+                nc.scalar.copy(
+                    out=gr[:].bitcast(F32).rearrange("p (g r u) -> p g r u", g=G, u=2),
+                    in_=turned[c][:].rearrange("p (g u) r -> p g r u", u=2),
+                )
             grouped[c] = gr
 
         def quant(c):
-            co = stage.tile([P, G * P], U32, name="co", bufs=6, align_bytes=64)
-            sc = stage.tile([P, G * P], U8, name="sc", bufs=6, align_bytes=64)
+            co = stage.tile([P, G * P], U32, name="co", align_bytes=64)
+            sc = stage.tile([P, G * P], U8, name="sc", align_bytes=64)
             nc.vector.quantize_mx(out=co[:].bitcast(FP8X4), scales=sc[:], in_=grouped[c][:])
-            codes[c], scs[c] = co, sc
+            codes[c], scales[c] = co, sc
 
-        def project(c):
-            for n in range(2):
-                vp = psum.tile([P, 512], F32, name="vp", bufs=4)
-                for g in range(G):
-                    nc.tensor.matmul_mx(
-                        out=vp[:],
-                        lhsT=codes[c][:, P * g : P * (g + 1)].bitcast(FP8X4),
-                        lhsT_scale=scs[c][:, P * g : P * (g + 1)],
-                        rhs=wv[:, g, 1024 * n : 1024 * (n + 1)].bitcast(FP4X4),
-                        rhs_scale=wv_sc[:, g, 512 * n : 512 * (n + 1)],
-                        start=(g == 0),
-                        stop=(g == G - 1),
-                    )
-                vps[c, n] = vp
-
-        def split_hi(c):
-            hi = stage.tile([P, D], BF16, name="hi", bufs=6, align_bytes=64)
-            for n in range(2):
-                nc.scalar.copy(out=hi[:, 512 * n : 512 * (n + 1)], in_=vps[c, n][:])
-            his[c] = hi
-
-        def split_lo(c):
-            lo = stage.tile([P, D], BF16, name="lo", bufs=6, align_bytes=64)
-            for n in range(2):
-                cols = slice(512 * n, 512 * (n + 1))
-                nc.vector.tensor_tensor(out=lo[:, cols], in0=vps[c, n][:], in1=his[c][:, cols], op=SUB)
-            los[c] = lo
-
-        batch_of = {c: bt for bt, (c0, c1) in enumerate(BATCHES) for c in range(c0, c1)}
-
-        def pool(c):
-            bt = batch_of[c]
-            c0, c1 = BATCHES[bt]
-            if c == c0:
-                po = psum.tile([P, c1 - c0, NB, BF, 2], F32, name="po", bufs=2)
-                pools[bt] = po
-            for b in range(NB):
-                ch = slice(128 * b, 128 * (b + 1))
-                for part, start in ((his, True), (los, False)):
-                    nc.tensor.matmul(
-                        pools[bt][:, c - c0, b, :, :],
-                        lhsT=part[c][:, ch],
-                        rhs=lw[:, :, c, b, :],
-                        start=start,
-                        stop=not start,
-                    )
-
-        def pick(bt, copy):
-            c0, c1 = BATCHES[bt]
-            for hh in range(2):
-                rows = slice(64 * hh, 64 * (hh + 1))
-                dst = attn_t[rows, :, :].rearrange("q b (f c) -> q b f c", f=BF)
-                copy(
-                    out=dst[:, :, :, c0:c1],
-                    in_=pools[bt][rows, :, :, :, hh].rearrange("q c b f -> q b f c"),
-                )
-
-        def permute(bt):
-            c0, c1 = BATCHES[bt]
-            pe = psum.tile([P, 4, G, BF, c1 - c0], F32, name="tr", bufs=2)
-            src = attn_t[:].rearrange("q (g j) (f c) -> q j g f c", g=G, f=BF)
-            for t in range(4):
-                for j in range(4):
-                    nc.tensor.matmul(
-                        pe[:, t, :, :, :],
-                        lhsT=perm[:, t, 96 - 32 * j : 224 - 32 * j],
-                        rhs=src[:, j, :, :, c0:c1],
-                        start=(j == 0),
-                        stop=(j == 3),
-                    )
-            perms[bt] = pe
-
-        def interleave(bt, copy):
-            c0, c1 = BATCHES[bt]
-            dst = attn_k[:].rearrange("p g (f c) t -> p (g f) c t", f=BF)
-            copy(
-                out=dst[:, :, c0:c1, :],
-                in_=perms[bt][:].rearrange("p t g f c -> p (g f) c t"),
-            )
-
-        nc.scalar.copy(out=perm[:, :, 96:128], in_=ident[:].rearrange("q (r t) -> q t r", t=4))
-        nc.vector.tensor_reduce(
-            out=mask[:], in_=ident[:].rearrange("p (q f) -> p f q", f=BF), axis=AXIS_X, op=ADD
-        )
-        for f in range(BF):
-            nc.scalar.activation(
-                out=lw[:, f, :, :, :].rearrange("p c b h -> p (c b h)"),
-                in_=logw_sb[:],
-                func=mybir.ActivationFunctionType.Copy,
-                scale=mask[:, f : f + 1],
-            )
-
-        def on(fn, c):
-            if 0 <= c < NT:
-                fn(c)
-
-        def both(fn, p, lead, shift=0):
-            for c in (2 * (p + lead) - shift, 2 * (p + lead) + 1 - shift):
-                if 0 <= c < NT:
-                    fn(c)
-
-        def products(p):
-            if 0 <= p < NT // 2:
-                widen(2 * p)
-                if p < FIRST_SHARED:
-                    widen(2 * p + 1)
-                else:
-                    widen(2 * p + 1, PW, D)
-
-        def shared(fn, p):
-            if FIRST_SHARED <= p < NT // 2:
-                fn(2 * p + 1)
-
-        def mark(c):
-            nc.vector.memset(xs[c][:, :16], 0.0)
-
-        for c in range(6):
-            new_x(c)
-        widen(0, 0, 512)
-        widen(0, 512, D)
-        widen(1)
-        turn(0)
-        gather(0)
-        turn(1)
-        gather(1)
-        widen(2)
-        quant(0)
-        widen(3)
-        quant(1)
-        project(0)
-        turn(2)
-        project(1)
-        turn(3)
-        split_hi(0)
-        gather(2)
-        split_hi(1)
-        gather(3)
-        widen(4)
-        widen(5)
-        cast(7)
-        for p in range(NT // 2):
-            both(new_x, p, 3)
-            both(project, p, 0) if p > 0 else None
-            both(turn, p, 2)
-            both(split_hi, p, 0) if p > 0 else None
-            both(gather, p, 2)
-            products(p + 3)
-            both(quant, p, 1)
-            shared(mark, p + 3)
-            shared(widen_on_pool, p + 3)
-            both(split_lo, p, 0)
-            shared(cast, p + 4)
-            both(pool, p, 0, 2)
-            if p in (4, 8, 12):
-                pick((p - 4) // 4, nc.scalar.copy)
-            if p in (5, 9, 13):
-                permute((p - 5) // 4)
-                interleave((p - 5) // 4, nc.scalar.copy)
-        pick(3, nc.scalar.copy)
-        pool(30)
-        pool(31)
-        pick(4, nc.vector.tensor_copy)
-        permute(3)
-        interleave(3, nc.scalar.copy)
-        permute(4)
-        interleave(4, nc.vector.tensor_copy)
-        nc.vector.quantize_mx(
-            out=attn_codes[:].bitcast(FP8X4),
-            scales=attn_sc[:],
-            in_=attn_k[:].rearrange("p g b t -> p (g b t)"),
-        )
-        for n in range(2):
-            acc = psum.tile([P, 512], F32, name="vp", bufs=4)
+        def multiply_mx(acc, words, word_scales, w, w_scales, n):
             for g in range(G):
+                rows = slice(P * g, P * (g + 1))
                 nc.tensor.matmul_mx(
                     out=acc[:],
-                    lhsT=attn_codes[:, 128 * g : 128 * (g + 1)].bitcast(FP8X4),
-                    lhsT_scale=attn_sc[:, 128 * g : 128 * (g + 1)],
-                    rhs=wo[:, g, 1024 * n : 1024 * (n + 1)].bitcast(FP4X4),
-                    rhs_scale=wo_sc[:, g, 512 * n : 512 * (n + 1)],
+                    lhsT=words[:, rows].bitcast(FP8X4),
+                    lhsT_scale=word_scales[:, rows],
+                    rhs=w[:, g, 2 * PASS * n : 2 * PASS * (n + 1)].bitcast(FP4X4),
+                    rhs_scale=w_scales[:, g, PASS * n : PASS * (n + 1)],
                     start=(g == 0),
                     stop=(g == G - 1),
                 )
-            res = keep.tile([P, 512], F32, name="res%d" % n)
-            if n == 0:
-                nc.scalar.copy(out=res[:], in_=acc[:])
-            else:
-                nc.vector.tensor_copy(out=res[:], in_=acc[:])
-            nc.sync.dma_start(out=out[:, 512 * n : 512 * (n + 1)], in_=res[:])
+
+        def project(c):
+            for n in range(2):
+                acc = psum.tile([P, PASS], F32, name="acc", bufs=4)
+                multiply_mx(acc, codes[c], scales[c], wv, wv_scales, n)
+                vp[c, n] = acc
+
+        def split_hi(c):
+            h = stage.tile([P, D], BF16, name="h", align_bytes=64)
+            for n in range(2):
+                nc.scalar.copy(out=h[:, PASS * n : PASS * (n + 1)], in_=vp[c, n][:])
+            hi[c] = h
+
+        def split_lo(c):
+            rest = stage.tile([P, D], BF16, name="rest", align_bytes=64)
+            for n in range(2):
+                cols = slice(PASS * n, PASS * (n + 1))
+                nc.vector.tensor_tensor(out=rest[:, cols], in0=vp[c, n][:], in1=hi[c][:, cols], op=SUB)
+            lo[c] = rest
+
+        group_of = {c: k for k, (c0, c1) in enumerate(BATCHES) for c in range(c0, c1)}
+
+        def pool(c):
+            k = group_of[c]
+            c0, c1 = BATCHES[k]
+            if c == c0:
+                bank = psum.tile([P, c1 - c0, BF, NB, HB], F32, name="bank", bufs=2)
+                sums[k] = bank
+            for b in range(NB):
+                blocks = slice(b, min(b + POOL_BLOCKS, NB))
+                for part, first in ((hi, True), (lo, False)):
+                    nc.tensor.matmul(
+                        sums[k][:, c - c0, :, blocks, :],
+                        lhsT=part[c][:, P * b : P * (b + 1)],
+                        rhs=weights[:, :, c, blocks, :],
+                        start=first,
+                        stop=not first,
+                    )
+
+        def pick(k, copy):
+            for hh in range(HB):
+                rows = slice(64 * hh, 64 * (hh + 1))
+                copy(
+                    out=pooled[k][rows, :, :, :],
+                    in_=sums[k][rows, :, :, :, hh].rearrange("q c f b -> q b f c"),
+                )
+
+        def reorder(k):
+            c0, c1 = BATCHES[k]
+            bank = psum.tile([P, T, G, BF * (c1 - c0)], F32, name="tr", bufs=2)
+            blocks = pooled[k][:].rearrange("q (g j) f c -> q j g (f c)", g=G)
+            for t in range(T):
+                for j in range(4):
+                    nc.tensor.matmul(
+                        bank[:, t, :, :],
+                        lhsT=move[:, t, 96 - 32 * j : 224 - 32 * j],
+                        rhs=blocks[:, j, :, :],
+                        start=(j == 0),
+                        stop=(j == 3),
+                    )
+            moved[k] = bank
+
+        def interleave(k, copy):
+            c0, c1 = BATCHES[k]
+            copy(
+                out=attn[:].rearrange("p g (f c) t -> p (g f) c t", f=BF)[:, :, c0:c1, :],
+                in_=moved[k][:].rearrange("p t g (f c) -> p (g f) c t", f=BF),
+            )
+
+        def pair(step, p, shift=0):
+            for c in (2 * p - shift, 2 * p + 1 - shift):
+                if 0 <= c < NT:
+                    step(c)
+
+        for c in range(6):
+            new_product(c)
+        nc.vector.tensor_copy(out=product[0][:], in_=tile_bytes[0].bitcast(FP8))
+        nc.scalar.copy(out=product[1][:], in_=tile_bytes[1].bitcast(FP8))
+        for f in range(BF):
+            nc.gpsimd.tensor_scalar(
+                out=weights[:, f, :, :, :].rearrange("p c b h -> p (c b h)"),
+                in0=logw_sb[:],
+                scalar1=is_row[:, f : f + 1],
+                scalar2=0.0,
+                op0=MULT,
+                op1=ADD,
+            )
+        turn(0)
+        gather(0)
+        turn(1)
+        quant(0)
+        gather(1)
+        quant(1)
+        multiply(2)
+        project(0)
+        turn(2)
+        nc.scalar.copy(out=move[:, :, 96:128], in_=ident[:].rearrange("q (r t) -> q t r", t=T))
+        multiply(3)
+        split_hi(0)
+        gather(2)
+        project(1)
+        turn(3)
+        split_hi(1)
+        gather(3)
+        widen(2 * FIRST_SHARED + 1)
+
+        for p in range(PAIRS):
+            pair(new_product, p + 3)
+            if p + 2 < PAIRS:
+                multiply(2 * p + 4)
+                multiply(2 * p + 5, SHARE if p + 2 >= FIRST_SHARED else 0)
+            if p > 0:
+                pair(project, p)
+            pair(turn, p + 2)
+            if p > 0:
+                pair(split_hi, p)
+            pair(gather, p + 2)
+            pair(quant, p + 1)
+            if FIRST_SHARED <= p + 3 < PAIRS:
+                multiply_on_gpsimd(2 * p + 7)
+            pair(split_lo, p)
+            if p + 4 < PAIRS:
+                widen(2 * p + 9)
+            pair(pool, p, shift=2)
+            if p in (3, 6, 9, 12):
+                pick(p // 3 - 1, nc.scalar.copy)
+            if p in (4, 7, 10, 13):
+                reorder(p // 3 - 1)
+                interleave(p // 3 - 1, nc.scalar.copy)
+
+        pick(4, nc.scalar.copy)
+        pair(pool, PAIRS - 1)
+        pick(5, nc.vector.tensor_copy)
+        reorder(4)
+        interleave(4, nc.scalar.copy)
+        reorder(5)
+        interleave(5, nc.vector.tensor_copy)
+        nc.vector.quantize_mx(
+            out=attn_codes[:].bitcast(FP8X4),
+            scales=attn_scales[:],
+            in_=attn[:].rearrange("p g b t -> p (g b t)"),
+        )
+        for n, copy in ((0, nc.scalar.copy), (1, nc.vector.tensor_copy)):
+            acc = psum.tile([P, PASS], F32, name="acc", bufs=4)
+            multiply_mx(acc, attn_codes, attn_scales, wo, wo_scales, n)
+            result = keep.tile([P, PASS], F32, name="result%d" % n)
+            copy(out=result[:], in_=acc[:])
+            nc.sync.dma_start(out=out[:, PASS * n : PASS * (n + 1)], in_=result[:])

from contextlib import ExitStack

import concourse.mybir as mybir
from concourse.masks import make_identity

F32 = mybir.dt.float32
BF16 = mybir.dt.bfloat16
U32 = mybir.dt.uint32
I32 = mybir.dt.int32
U8 = mybir.dt.uint8
FP8 = mybir.dt.float8_e4m3fn
FP8X4 = mybir.dt.float8_e4m3fn_x4
FP4X4 = mybir.dt.float4_e2m1fn_x4
MULT = mybir.AluOpType.mult
ADD = mybir.AluOpType.add
SUB = mybir.AluOpType.subtract
AXIS_X = mybir.AxisListType.X

SEQ, BATCH, D, HEADS = 32, 128, 1024, 16

P = 128
G = 2
PASS = 512
T = 4
NT = 32
PAIRS = NT // 2
BF = 4
NB = 8
HB = 2

BATCHES = ((0, 6), (6, 12), (12, 18), (18, 24), (24, 30), (30, 32))

POOL_BLOCKS = 3

SCALED_LATE = (0, 1)

FIRST_SHARED = 3
SHARE = 640

FLOPS = 2 * SEQ * BATCH * D * D + 2 * BATCH * D * D


def tile_multiheadattention_pb_w4_kernel(
    tc, values_bytes, values_scale, logw, Wv_words, Wv_scales, Wo_words, Wo_scales, out
):
    nc = tc.nc
    with ExitStack() as ctx:
        keep = ctx.enter_context(tc.tile_pool(name="keep", bufs=1))
        stage = ctx.enter_context(tc.tile_pool(name="stage", bufs=6))
        psum = ctx.enter_context(tc.psum_pool(name="psum", bufs=2))
        ctx.enter_context(tc.manual_schedule())

        factors = keep.tile([P, D], F32, name="factors")
        factors_k = keep.tile([P, G, T], F32, name="factors_k")
        logw_sb = keep.tile([P, NT * HEADS], BF16, name="logw_sb")
        wv = keep.tile([P, G, 2 * D], U8, name="wv", align_bytes=64)
        wo = keep.tile([P, G, 2 * D], U8, name="wo", align_bytes=64)
        wv_scales = keep.tile([P, G, D], U8, name="wv_scales", align_bytes=64)
        wo_scales = keep.tile([P, G, D], U8, name="wo_scales", align_bytes=64)
        ident = keep.tile([P, P], F32, name="ident", align_bytes=64)
        is_row = keep.tile([P, BF], F32, name="is_row")
        weights = keep.tile([P, BF, NT, NB, HB], BF16, name="weights", align_bytes=64)
        move = keep.tile([P, T, 224], BF16, name="move", align_bytes=64)
        pooled = [
            keep.tile([P, NB, BF, c1 - c0], BF16, name="pooled%d" % c0, align_bytes=64) for c0, c1 in BATCHES
        ]
        attn = keep.tile([P, G, BATCH, T], BF16, name="attn", align_bytes=64)
        attn_codes = keep.tile([P, G * BATCH], U32, name="attn_codes", align_bytes=64)
        attn_scales = keep.tile([P, G * BATCH], U8, name="attn_scales", align_bytes=64)

        nc.gpsimd.memset(wv_scales[:].rearrange("p g n -> p (g n)").bitcast(I32), 0)
        make_identity(nc, ident[:])
        nc.gpsimd.memset(wo_scales[:].rearrange("p g n -> p (g n)").bitcast(I32), 0)
        nc.gpsimd.memset(move[:], 0.0)
        nc.vector.tensor_reduce(
            out=is_row[:], in_=ident[:].rearrange("p (q f) -> p f q", f=BF), axis=AXIS_X, op=ADD
        )

        tokens = values_bytes.flatten_outer_dims().rearrange("(i c) k -> i c k", c=NT)
        tile_bytes = {}

        def load_values(c0, c1):
            codes_in = keep.tile([P, c1 - c0, D], U8, name="codes_in%d" % c0, align_bytes=64)
            nc.sync.dma_start(out=codes_in[:], in_=tokens[:, c0:c1, :])
            for c in range(c0, c1):
                tile_bytes[c] = codes_in[:, c - c0, :]

        def load_weight_scales(dst, src):
            for r in range(4):
                nc.sync.dma_start(
                    out=dst[:].bitcast(I32)[r:P:32, :, :],
                    in_=src.bitcast(I32)[:, r::4, :].rearrange("g q n -> q g n"),
                )

        load_values(0, 1)
        nc.sync.dma_start(
            out=factors_k[:], in_=values_scale.rearrange("a o (g p t) -> p (a o g) t", g=G, t=T)
        )
        load_values(1, 2)
        nc.sync.dma_start(
            out=factors[:], in_=values_scale.rearrange("a o k -> (a o k)").partition_broadcast(P)
        )
        nc.sync.dma_start(
            out=logw_sb[:], in_=logw.flatten_outer_dims().rearrange("(i c) h -> i (c h)", c=NT)
        )
        load_values(2, 4)
        nc.sync.dma_start(out=wv[:], in_=Wv_words.rearrange("g p x -> p g x"))
        load_weight_scales(wv_scales, Wv_scales)
        for c0 in range(4, NT, 4):
            load_values(c0, c0 + 4)
        nc.sync.dma_start(out=wo[:], in_=Wo_words.rearrange("g p x -> p g x"))
        load_weight_scales(wo_scales, Wo_scales)

        product, plain, turned, grouped, codes, scales = {}, {}, {}, {}, {}, {}
        vp, hi, lo, sums, moved = {}, {}, {}, {}, {}

        def new_product(c):
            x = stage.tile([P, D], BF16, name="x", bufs=14, align_bytes=64)
            product[c] = x

        def multiply(c, k0=0):
            nc.vector.tensor_tensor(
                out=product[c][:, k0:], in0=tile_bytes[c][:, k0:].bitcast(FP8), in1=factors[:, k0:], op=MULT
            )

        def widen(c):
            xc = stage.tile([P, SHARE], BF16, name="xc", bufs=3, align_bytes=64)
            nc.scalar.copy(out=xc[:], in_=tile_bytes[c][:, :SHARE].bitcast(FP8))
            plain[c] = xc

        def multiply_on_gpsimd(c):
            nc.vector.memset(product[c][:, :16], 0.0)
            nc.gpsimd.tensor_tensor(out=product[c][:, :SHARE], in0=plain[c][:], in1=factors[:, :SHARE], op=MULT)

        def turn(c):
            tr = psum.tile([P, 2 * G, P], F32, name="tr", bufs=2)
            words = product[c][:].bitcast(F32)
            for g in range(G):
                for u in range(2):
                    nc.tensor.transpose(
                        tr[:, 2 * g + u, :], words[:, 256 * g + u : 256 * (g + 1) : 2], ident[:]
                    )
            turned[c] = tr

        def gather(c):
            gr = stage.tile([P, D], BF16, name="gr", align_bytes=64)
            if c in SCALED_LATE:
                for g in range(G):
                    values = turned[c][:, 2 * g : 2 * (g + 1), :].rearrange("p u r -> p (u r)").bitcast(BF16)
                    factor = factors_k[:, g, :].unsqueeze(1).to_broadcast([P, P, T])
                    nc.vector.tensor_tensor(
                        out=gr[:, PASS * g : PASS * (g + 1)].rearrange("p (r u e) -> p r u e", u=2, e=2),
                        in0=values.rearrange("p (u r e) -> p r u e", u=2, e=2),
                        in1=factor.rearrange("p r (u e) -> p r u e", u=2),
                        op=MULT,
                    )
            else:
                nc.scalar.copy(
                    out=gr[:].bitcast(F32).rearrange("p (g r u) -> p g r u", g=G, u=2),
                    in_=turned[c][:].rearrange("p (g u) r -> p g r u", u=2),
                )
            grouped[c] = gr

        def quant(c):
            co = stage.tile([P, G * P], U32, name="co", align_bytes=64)
            sc = stage.tile([P, G * P], U8, name="sc", align_bytes=64)
            nc.vector.quantize_mx(out=co[:].bitcast(FP8X4), scales=sc[:], in_=grouped[c][:])
            codes[c], scales[c] = co, sc

        def multiply_mx(acc, words, word_scales, w, w_scales, n):
            for g in range(G):
                rows = slice(P * g, P * (g + 1))
                nc.tensor.matmul_mx(
                    out=acc[:],
                    lhsT=words[:, rows].bitcast(FP8X4),
                    lhsT_scale=word_scales[:, rows],
                    rhs=w[:, g, 2 * PASS * n : 2 * PASS * (n + 1)].bitcast(FP4X4),
                    rhs_scale=w_scales[:, g, PASS * n : PASS * (n + 1)],
                    start=(g == 0),
                    stop=(g == G - 1),
                )

        def project(c):
            for n in range(2):
                acc = psum.tile([P, PASS], F32, name="acc", bufs=4)
                multiply_mx(acc, codes[c], scales[c], wv, wv_scales, n)
                vp[c, n] = acc

        def split_hi(c):
            h = stage.tile([P, D], BF16, name="h", align_bytes=64)
            for n in range(2):
                nc.scalar.copy(out=h[:, PASS * n : PASS * (n + 1)], in_=vp[c, n][:])
            hi[c] = h

        def split_lo(c):
            rest = stage.tile([P, D], BF16, name="rest", align_bytes=64)
            for n in range(2):
                cols = slice(PASS * n, PASS * (n + 1))
                nc.vector.tensor_tensor(out=rest[:, cols], in0=vp[c, n][:], in1=hi[c][:, cols], op=SUB)
            lo[c] = rest

        group_of = {c: k for k, (c0, c1) in enumerate(BATCHES) for c in range(c0, c1)}

        def pool(c):
            k = group_of[c]
            c0, c1 = BATCHES[k]
            if c == c0:
                bank = psum.tile([P, c1 - c0, BF, NB, HB], F32, name="bank", bufs=2)
                sums[k] = bank
            for b in range(NB):
                blocks = slice(b, min(b + POOL_BLOCKS, NB))
                for part, first in ((hi, True), (lo, False)):
                    nc.tensor.matmul(
                        sums[k][:, c - c0, :, blocks, :],
                        lhsT=part[c][:, P * b : P * (b + 1)],
                        rhs=weights[:, :, c, blocks, :],
                        start=first,
                        stop=not first,
                    )

        def pick(k, copy):
            for hh in range(HB):
                rows = slice(64 * hh, 64 * (hh + 1))
                copy(
                    out=pooled[k][rows, :, :, :],
                    in_=sums[k][rows, :, :, :, hh].rearrange("q c f b -> q b f c"),
                )

        def reorder(k):
            c0, c1 = BATCHES[k]
            bank = psum.tile([P, T, G, BF * (c1 - c0)], F32, name="tr", bufs=2)
            blocks = pooled[k][:].rearrange("q (g j) f c -> q j g (f c)", g=G)
            for t in range(T):
                for j in range(4):
                    nc.tensor.matmul(
                        bank[:, t, :, :],
                        lhsT=move[:, t, 96 - 32 * j : 224 - 32 * j],
                        rhs=blocks[:, j, :, :],
                        start=(j == 0),
                        stop=(j == 3),
                    )
            moved[k] = bank

        def interleave(k, copy):
            c0, c1 = BATCHES[k]
            copy(
                out=attn[:].rearrange("p g (f c) t -> p (g f) c t", f=BF)[:, :, c0:c1, :],
                in_=moved[k][:].rearrange("p t g (f c) -> p (g f) c t", f=BF),
            )

        def pair(step, p, shift=0):
            for c in (2 * p - shift, 2 * p + 1 - shift):
                if 0 <= c < NT:
                    step(c)

        for c in range(6):
            new_product(c)
        nc.vector.tensor_copy(out=product[0][:], in_=tile_bytes[0].bitcast(FP8))
        nc.scalar.copy(out=product[1][:], in_=tile_bytes[1].bitcast(FP8))
        for f in range(BF):
            nc.gpsimd.tensor_scalar(
                out=weights[:, f, :, :, :].rearrange("p c b h -> p (c b h)"),
                in0=logw_sb[:],
                scalar1=is_row[:, f : f + 1],
                scalar2=0.0,
                op0=MULT,
                op1=ADD,
            )
        turn(0)
        gather(0)
        turn(1)
        quant(0)
        gather(1)
        quant(1)
        multiply(2)
        project(0)
        turn(2)
        nc.scalar.copy(out=move[:, :, 96:128], in_=ident[:].rearrange("q (r t) -> q t r", t=T))
        multiply(3)
        split_hi(0)
        gather(2)
        project(1)
        turn(3)
        split_hi(1)
        gather(3)
        widen(2 * FIRST_SHARED + 1)

        for p in range(PAIRS):
            pair(new_product, p + 3)
            if p + 2 < PAIRS:
                multiply(2 * p + 4)
                multiply(2 * p + 5, SHARE if p + 2 >= FIRST_SHARED else 0)
            if p > 0:
                pair(project, p)
            pair(turn, p + 2)
            if p > 0:
                pair(split_hi, p)
            pair(gather, p + 2)
            pair(quant, p + 1)
            if FIRST_SHARED <= p + 3 < PAIRS:
                multiply_on_gpsimd(2 * p + 7)
            pair(split_lo, p)
            if p + 4 < PAIRS:
                widen(2 * p + 9)
            pair(pool, p, shift=2)
            if p in (3, 6, 9, 12):
                pick(p // 3 - 1, nc.scalar.copy)
            if p in (4, 7, 10, 13):
                reorder(p // 3 - 1)
                interleave(p // 3 - 1, nc.scalar.copy)

        pick(4, nc.scalar.copy)
        pair(pool, PAIRS - 1)
        pick(5, nc.vector.tensor_copy)
        reorder(4)
        interleave(4, nc.scalar.copy)
        reorder(5)
        interleave(5, nc.vector.tensor_copy)
        nc.vector.quantize_mx(
            out=attn_codes[:].bitcast(FP8X4),
            scales=attn_scales[:],
            in_=attn[:].rearrange("p g b t -> p (g b t)"),
        )
        for n, copy in ((0, nc.scalar.copy), (1, nc.vector.tensor_copy)):
            acc = psum.tile([P, PASS], F32, name="acc", bufs=4)
            multiply_mx(acc, attn_codes, attn_scales, wo, wo_scales, n)
            result = keep.tile([P, PASS], F32, name="result%d" % n)
            copy(out=result[:], in_=acc[:])
            nc.sync.dma_start(out=out[:, PASS * n : PASS * (n + 1)], in_=result[:])
